import numpy as np
import ml_dtypes

BF16 = ml_dtypes.bfloat16


def bf(x):
    return np.asarray(x, np.float32).astype(BF16)


def f32(x):
    return np.asarray(x, np.float32)


def f64(x):
    return np.asarray(x).astype(np.float64)


def striped(idx):
    return np.tile(idx.reshape(-1, 16).T, (8, 1))


T, NN, S, N, H, NIN, FF = 8, 32, 1024, 8192, 128, 384, 512
EPS = 1e-6


def relu(v):
    return np.maximum(v, 0.0)


def normalize(x, gain, bias):
    mu = x.mean(axis=0, keepdims=True)
    sigma = np.sqrt(((x - mu) ** 2).sum(axis=0, keepdims=True) / (H - 1))
    return gain * (x - mu) / (sigma + EPS) + bias


def reverse_edges():
    rows = np.arange(NN)[:, None]
    pieces = []
    for _ in range(T):
        nb = np.stack([np.random.permutation(NN) for _ in range(NN)])
        pos = np.zeros((NN, NN), np.int64)
        pos[rows, nb] = np.arange(NN)[None, :]
        pieces.append((nb * NN + pos[nb, rows]).reshape(-1))
    return np.concatenate(pieces)


def setup_inputs():
    return {
        "h_EV": bf(np.random.standard_normal((T, NIN, S))),
        "h_E": f32(np.random.standard_normal((H, N))),
        "w1": bf(np.random.standard_normal((NIN, H)) * np.sqrt(2.0 / NIN)),
        "b1": f32(0.1 * np.random.standard_normal((H, 1))),
        "w2": bf(np.random.standard_normal((H, H)) * np.sqrt(2.0 / H)),
        "b2": f32(0.1 * np.random.standard_normal((H, 1))),
        "w3": bf(np.random.standard_normal((H, H)) / np.sqrt(H)),
        "b3": f32(0.1 * np.random.standard_normal((H, 1))),
        "ffn_w_in": bf(np.random.standard_normal((H, FF)) * np.sqrt(2.0 / H)),
        "ffn_b_in": f32(0.1 * np.random.standard_normal((FF, 1))),
        "ffn_w_out": bf(np.random.standard_normal((FF, H)) / np.sqrt(FF)),
        "ffn_b_out": f32(0.1 * np.random.standard_normal((H, 1))),
        "gain0": f32(1.0 + 0.1 * np.random.standard_normal((H, 1))),
        "bias0": f32(0.1 * np.random.standard_normal((H, 1))),
        "gain1": f32(1.0 + 0.1 * np.random.standard_normal((H, 1))),
        "bias1": f32(0.1 * np.random.standard_normal((H, 1))),
        "offs": striped(reverse_edges()),
    }


def reference(h_EV, h_E, w1, b1, w2, b2, w3, b3, ffn_w_in, ffn_b_in, ffn_w_out, ffn_b_out, gain0, bias0, gain1, bias1, offs):
    idx = offs[:16].T.reshape(-1)
    cols = []
    for t in range(T):
        a1 = relu(f64(w1).T @ f64(h_EV)[t] + f64(b1))
        a2 = relu(f64(w2).T @ a1 + f64(b2))
        piece = idx[t * S:(t + 1) * S]
        cols.append(0.5 * (f64(w3).T @ a2 + f64(w3).T @ a2[:, piece]) + f64(b3))
    dh = np.concatenate(cols, axis=1)
    u = normalize(f64(h_E) + dh, f64(gain0), f64(bias0))
    v = relu(f64(ffn_w_in).T @ u + f64(ffn_b_in))
    return normalize(u + f64(ffn_w_out).T @ v + f64(ffn_b_out), f64(gain1), f64(bias1))

@@ -1,0 +1,195 @@
+import concourse.mybir as mybir
+from concourse.masks import make_identity
+
+F32, BF16, U16 = mybir.dt.float32, mybir.dt.bfloat16, mybir.dt.uint16
+ACT = mybir.ActivationFunctionType
+ALU = mybir.AluOpType
+AXIS = mybir.AxisListType
+
+P = 128
+TERMS, EDGES = 8, 1024
+IN_BLOCKS = 3
+FF_BLOCKS = 4
+PIECE = 512
+PIECES = TERMS * EDGES // PIECE
+HALVES = EDGES // PIECE
+COL_BLOCKS = PIECE // P
+EPS = 1e-6
+SQRT_FLOOR = 1e-30
+
+FLOPS = 2 * TERMS * EDGES * P * (IN_BLOCKS * P + P + 2 * P + 2 * FF_BLOCKS * P)
+
+
+def tile_termedgempnnlayer_b_kernel(
+    tc, h_EV, h_E, w1, b1, w2, b2, w3, b3, ffn_w_in, ffn_b_in, ffn_w_out, ffn_b_out,
+    gain0, bias0, gain1, bias1, offs, out,
+):
+    nc = tc.nc
+    with (
+        tc.tile_pool(name="held", bufs=1) as held,
+        tc.tile_pool(name="loads", bufs=4) as loads,
+        tc.tile_pool(name="edges", bufs=TERMS) as edges,
+        tc.tile_pool(name="pieces", bufs=PIECES) as pieces,
+        tc.tile_pool(name="work", bufs=4) as work,
+        tc.tile_pool(name="small", bufs=4) as small,
+    ):
+        w1_sb = held.tile([P, IN_BLOCKS, P], BF16, name="w1_sb")
+        nc.scalar.dma_start(w1_sb[:], w1.rearrange("(a p) c -> p a c", p=P))
+
+        def load_column(vector, blocks, name):
+            column = held.tile([P, blocks], F32, name=name)
+            nc.scalar.dma_start(column[:], vector.rearrange("(a p) o -> p (a o)", p=P))
+            return column
+
+        b1_col = load_column(b1, 1, "b1_col")
+        w2_sb = held.tile([P, P], BF16, name="w2_sb")
+        nc.scalar.dma_start(w2_sb[:], w2)
+        b2_col = load_column(b2, 1, "b2_col")
+        offsets = held.tile([P, TERMS * EDGES // 16], U16, name="offsets")
+        nc.sync.dma_start(offsets[:], offs)
+        w3_sb = held.tile([P, P], BF16, name="w3_sb")
+        nc.scalar.dma_start(w3_sb[:], w3)
+        b3_col = load_column(b3, 1, "b3_col")
+        w_in_sb = held.tile([P, FF_BLOCKS * P], BF16, name="w_in_sb")
+        nc.scalar.dma_start(w_in_sb[:], ffn_w_in)
+        w_out_sb = held.tile([P, FF_BLOCKS, P], BF16, name="w_out_sb")
+        nc.scalar.dma_start(w_out_sb[:], ffn_w_out.rearrange("(a p) c -> p a c", p=P))
+        b_in_col = load_column(ffn_b_in, FF_BLOCKS, "b_in_col")
+        b_out_col = load_column(ffn_b_out, 1, "b_out_col")
+        gain0_col = load_column(gain0, 1, "gain0_col")
+        bias0_col = load_column(bias0, 1, "bias0_col")
+        gain1_col = load_column(gain1, 1, "gain1_col")
+        bias1_col = load_column(bias1, 1, "bias1_col")
+
+        minus_mean_bf = held.tile([P, P], BF16, name="minus_mean_bf")
+        nc.vector.memset(minus_mean_bf[:], -1.0 / P)
+        minus_mean_f32 = held.tile([P, P], F32, name="minus_mean_f32")
+        nc.vector.memset(minus_mean_f32[:], -1.0 / P)
+        ones_col = held.tile([P, 1], BF16, name="ones_col")
+        nc.vector.memset(ones_col[:], 1.0)
+        floor_col = held.tile([P, 1], F32, name="floor_col")
+        nc.vector.memset(floor_col[:], SQRT_FLOOR)
+        identity = held.tile([P, P], F32, name="identity")
+        make_identity(nc, identity[:])
+
+        def centre_rows(centred, weights, scale):
+            row_sum = small.tile([P, 1], F32, name="row_sum")
+            nc.vector.reduce_sum(row_sum[:], weights, axis=AXIS.X)
+            minus_row_mean = small.tile([P, 1], F32, name="minus_row_mean")
+            nc.vector.tensor_scalar_mul(minus_row_mean[:], row_sum[:], -1.0 / P)
+            nc.vector.tensor_scalar(centred, weights, minus_row_mean[:, 0:1], scale, ALU.add, ALU.mult)
+
+        w3_centred = held.tile([P, P], BF16, name="w3_centred")
+        centre_rows(w3_centred[:], w3_sb[:], 0.5)
+        w_out_centred = held.tile([P, FF_BLOCKS, P], BF16, name="w_out_centred")
+        for f in range(FF_BLOCKS):
+            centre_rows(w_out_centred[:, f, :], w_out_sb[:, f, :], 1.0)
+
+        a2 = [held.tile([P, EDGES], BF16, name="a2_%d" % t) for t in range(TERMS)]
+
+        with tc.psum_pool(name="psum_layers", bufs=3) as psum:
+            plain_cols = held.tile([P, 2], F32, name="plain_cols")
+            nc.vector.tensor_copy(plain_cols[:, 0:1], b3_col[:])
+            nc.vector.tensor_copy(plain_cols[:, 1:2], b_out_col[:])
+            minus_col_means = psum.tile([P, 2], F32, name="minus_col_means", bufs=1)
+            nc.tensor.matmul(minus_col_means[:], lhsT=minus_mean_f32[:], rhs=plain_cols[:], start=True, stop=True)
+            shifts = held.tile([P, 2], F32, name="shifts")
+            nc.vector.tensor_add(shifts[:], plain_cols[:], minus_col_means[:])
+            nc.vector.tensor_add(shifts[:, 1:2], shifts[:, 1:2], bias0_col[:])
+            x_shift, y_shift = shifts[:, 0:1], shifts[:, 1:2]
+
+            for t in range(TERMS):
+                h_ev = loads.tile([P, IN_BLOCKS, EDGES], BF16, name="h_ev")
+                nc.sync.dma_start(h_ev[:], h_EV[t].rearrange("(a p) e -> p a e", p=P))
+                for h in range(HALVES):
+                    cols = slice(h * PIECE, (h + 1) * PIECE)
+                    sum1 = psum.tile([P, PIECE], F32, name="sum1")
+                    for a in range(IN_BLOCKS):
+                        nc.tensor.matmul(sum1[:], lhsT=w1_sb[:, a, :], rhs=h_ev[:, a, cols],
+                                         start=(a == 0), stop=(a == IN_BLOCKS - 1))
+                    a1 = work.tile([P, PIECE], BF16, name="a1")
+                    nc.scalar.activation(a1[:], sum1[:], ACT.Relu, bias=b1_col[:, 0:1])
+                    sum2 = psum.tile([P, PIECE], F32, name="sum2")
+                    nc.tensor.matmul(sum2[:], lhsT=w2_sb[:], rhs=a1[:], start=True, stop=True)
+                    nc.vector.tensor_scalar(a2[t][:, cols], sum2[:], b2_col[:, 0:1], 0.0, ALU.add, ALU.max)
+
+        h_e = []
+        for t in range(TERMS):
+            h_e.append(edges.tile([P, EDGES], F32, name="h_e"))
+            nc.sync.dma_start(h_e[t][:], h_E[:, t * EDGES:(t + 1) * EDGES])
+
+        reverse_part = []
+        with tc.psum_pool(name="psum_gather", bufs=8) as psum:
+            for k in range(PIECES):
+                t, cols = k // HALVES, slice((k % HALVES) * PIECE, (k % HALVES + 1) * PIECE)
+                looked_up = a2[t][:].indirect(offsets[:, k * (PIECE // 16):(k + 1) * (PIECE // 16)])
+                reverse_sum = psum.tile([P, PIECE], F32, name="reverse_sum")
+                nc.tensor.matmul(reverse_sum[:], lhsT=w3_centred[:], rhs=looked_up, start=True, stop=True)
+                reverse_part.append(pieces.tile([P, PIECE], F32, name="reverse_part"))
+                nc.vector.scalar_tensor_tensor(reverse_part[k][:], reverse_sum[:], x_shift, h_e[t][:, cols],
+                                               ALU.add, ALU.add)
+
+        with tc.psum_pool(name="psum_rest", bufs=2) as psum:
+
+            def inverse_sigma(centred):
+                squares = work.tile([P, PIECE], BF16, name="squares")
+                nc.scalar.activation(squares[:], centred[:], ACT.Square)
+                square_sums = psum.tile([P, COL_BLOCKS], F32, name="square_sums", bufs=1)
+                for b in range(COL_BLOCKS):
+                    nc.tensor.matmul(square_sums[:, b:b + 1], lhsT=squares[:, b * P:(b + 1) * P], rhs=ones_col[:],
+                                     start=True, stop=True)
+                sigma = small.tile([P, COL_BLOCKS], F32, name="sigma")
+                nc.scalar.activation(sigma[:], square_sums[:], ACT.Sqrt, bias=floor_col[:, 0:1], scale=1.0 / (P - 1))
+                nc.vector.tensor_scalar_add(sigma[:], sigma[:], EPS)
+                inverse = small.tile([P, COL_BLOCKS], F32, name="inverse")
+                nc.vector.reciprocal(inverse[:], sigma[:])
+                spread = psum.tile([P, PIECE], F32, name="spread")
+                for b in range(COL_BLOCKS):
+                    nc.tensor.transpose(spread[:, b * P:(b + 1) * P], inverse[:, b:b + 1].to_broadcast([P, P]),
+                                        identity[:])
+                return spread
+
+            for k in range(PIECES):
+                t, cols = k // HALVES, slice((k % HALVES) * PIECE, (k % HALVES + 1) * PIECE)
+
+                h_e_bf = work.tile([P, PIECE], BF16, name="h_e_bf")
+                nc.gpsimd.tensor_scalar(h_e_bf[:], h_e[t][:, cols], 1.0, 0.0, ALU.mult, ALU.add)
+                forward_sum = psum.tile([P, PIECE], F32, name="forward_sum", tag="group")
+                nc.tensor.matmul(forward_sum[:], lhsT=minus_mean_bf[:], rhs=h_e_bf[:], start=True, stop=False)
+                nc.tensor.matmul(forward_sum[:], lhsT=w3_centred[:], rhs=a2[t][:, cols], start=False, stop=True)
+                x_centred = work.tile([P, PIECE], F32, name="x_centred")
+                nc.vector.tensor_add(x_centred[:], forward_sum[:], reverse_part[k][:])
+
+                x_scale = inverse_sigma(x_centred)
+                u_less_bias = work.tile([P, PIECE], F32, name="u_less_bias")
+                nc.vector.scalar_tensor_tensor(u_less_bias[:], x_centred[:], gain0_col[:, 0:1], x_scale[:],
+                                               ALU.mult, ALU.mult)
+                u_bf = work.tile([P, PIECE], BF16, name="u_bf")
+                nc.gpsimd.tensor_scalar(u_bf[:], u_less_bias[:], 1.0, bias0_col[:, 0:1], ALU.mult, ALU.add)
+
+                hidden = work.tile([P, FF_BLOCKS, PIECE], BF16, name="hidden")
+                for f in range(FF_BLOCKS):
+                    hidden_sum = psum.tile([P, PIECE], F32, name="hidden_sum", bufs=3)
+                    nc.tensor.matmul(hidden_sum[:], lhsT=w_in_sb[:, f * P:(f + 1) * P], rhs=u_bf[:],
+                                     start=True, stop=True)
+                    if f < FF_BLOCKS - 1:
+                        nc.scalar.activation(hidden[:, f, :], hidden_sum[:], ACT.Relu, bias=b_in_col[:, f:f + 1])
+                    else:
+                        nc.vector.tensor_scalar(hidden[:, f, :], hidden_sum[:], b_in_col[:, f:f + 1], 0.0,
+                                                ALU.add, ALU.max)
+
+                y_sum = psum.tile([P, PIECE], F32, name="y_sum", tag="group")
+                nc.tensor.matmul(y_sum[:], lhsT=minus_mean_bf[:], rhs=u_bf[:], start=True, stop=False)
+                for f in range(FF_BLOCKS):
+                    nc.tensor.matmul(y_sum[:], lhsT=w_out_centred[:, f, :], rhs=hidden[:, f, :],
+                                     start=False, stop=(f == FF_BLOCKS - 1))
+                y_centred = work.tile([P, PIECE], F32, name="y_centred")
+                nc.vector.scalar_tensor_tensor(y_centred[:], y_sum[:], y_shift, u_less_bias[:], ALU.add, ALU.add)
+
+                y_scale = inverse_sigma(y_centred)
+                scaled = work.tile([P, PIECE], F32, name="scaled")
+                nc.vector.scalar_tensor_tensor(scaled[:], y_centred[:], gain1_col[:, 0:1], y_scale[:],
+                                               ALU.mult, ALU.mult)
+                result = work.tile([P, PIECE], F32, name="result")
+                nc.gpsimd.tensor_scalar(result[:], scaled[:], 1.0, bias1_col[:, 0:1], ALU.mult, ALU.add)
+                nc.sync.dma_start(out[:, k * PIECE:(k + 1) * PIECE], result[:])

@@ -20,6 +20,15 @@ SQRT_FLOOR = 1e-30
 FLOPS = 2 * TERMS * EDGES * P * (IN_BLOCKS * P + P + 2 * P + 2 * FF_BLOCKS * P)
 
 
+def term_and_columns(k):
+    return k // HALVES, slice((k % HALVES) * PIECE, (k % HALVES + 1) * PIECE)
+
+
+def call_if_piece(step, k):
+    if 0 <= k < PIECES:
+        step(k)
+
+
 def tile_termedgempnnlayer_b_kernel(
     tc, h_EV, h_E, w1, b1, w2, b2, w3, b3, ffn_w_in, ffn_b_in, ffn_w_out, ffn_b_out,
     gain0, bias0, gain1, bias1, offs, out,
@@ -28,36 +37,35 @@ def tile_termedgempnnlayer_b_kernel(
     with (
         tc.tile_pool(name="held", bufs=1) as held,
         tc.tile_pool(name="loads", bufs=4) as loads,
-        tc.tile_pool(name="edges", bufs=TERMS) as edges,
         tc.tile_pool(name="pieces", bufs=PIECES) as pieces,
         tc.tile_pool(name="work", bufs=4) as work,
         tc.tile_pool(name="small", bufs=4) as small,
     ):
-        w1_sb = held.tile([P, IN_BLOCKS, P], BF16, name="w1_sb")
-        nc.scalar.dma_start(w1_sb[:], w1.rearrange("(a p) c -> p a c", p=P))
+        offsets = held.tile([P, TERMS * EDGES // 16], U16, name="offsets")
+        nc.sync.dma_start(offsets[:], offs)
 
         def load_column(vector, blocks, name):
             column = held.tile([P, blocks], F32, name=name)
             nc.scalar.dma_start(column[:], vector.rearrange("(a p) o -> p (a o)", p=P))
             return column
 
+        b3_col = load_column(b3, 1, "b3_col")
+        b_out_col = load_column(ffn_b_out, 1, "b_out_col")
+        bias0_col = load_column(bias0, 1, "bias0_col")
+        w1_sb = held.tile([P, IN_BLOCKS, P], BF16, name="w1_sb")
+        nc.scalar.dma_start(w1_sb[:], w1.rearrange("(a p) c -> p a c", p=P))
         b1_col = load_column(b1, 1, "b1_col")
         w2_sb = held.tile([P, P], BF16, name="w2_sb")
         nc.scalar.dma_start(w2_sb[:], w2)
         b2_col = load_column(b2, 1, "b2_col")
-        offsets = held.tile([P, TERMS * EDGES // 16], U16, name="offsets")
-        nc.sync.dma_start(offsets[:], offs)
         w3_sb = held.tile([P, P], BF16, name="w3_sb")
         nc.scalar.dma_start(w3_sb[:], w3)
-        b3_col = load_column(b3, 1, "b3_col")
         w_in_sb = held.tile([P, FF_BLOCKS * P], BF16, name="w_in_sb")
         nc.scalar.dma_start(w_in_sb[:], ffn_w_in)
         w_out_sb = held.tile([P, FF_BLOCKS, P], BF16, name="w_out_sb")
         nc.scalar.dma_start(w_out_sb[:], ffn_w_out.rearrange("(a p) c -> p a c", p=P))
         b_in_col = load_column(ffn_b_in, FF_BLOCKS, "b_in_col")
-        b_out_col = load_column(ffn_b_out, 1, "b_out_col")
         gain0_col = load_column(gain0, 1, "gain0_col")
-        bias0_col = load_column(bias0, 1, "bias0_col")
         gain1_col = load_column(gain1, 1, "gain1_col")
         bias1_col = load_column(bias1, 1, "bias1_col")
 
@@ -69,6 +77,8 @@ def tile_termedgempnnlayer_b_kernel(
         nc.vector.memset(ones_col[:], 1.0)
         floor_col = held.tile([P, 1], F32, name="floor_col")
         nc.vector.memset(floor_col[:], SQRT_FLOOR)
+        eps_col = held.tile([P, 1], F32, name="eps_col")
+        nc.vector.memset(eps_col[:], EPS)
         identity = held.tile([P, P], F32, name="identity")
         make_identity(nc, identity[:])
 
@@ -79,15 +89,10 @@ def tile_termedgempnnlayer_b_kernel(
             nc.vector.tensor_scalar_mul(minus_row_mean[:], row_sum[:], -1.0 / P)
             nc.vector.tensor_scalar(centred, weights, minus_row_mean[:, 0:1], scale, ALU.add, ALU.mult)
 
-        w3_centred = held.tile([P, P], BF16, name="w3_centred")
-        centre_rows(w3_centred[:], w3_sb[:], 0.5)
-        w_out_centred = held.tile([P, FF_BLOCKS, P], BF16, name="w_out_centred")
-        for f in range(FF_BLOCKS):
-            centre_rows(w_out_centred[:, f, :], w_out_sb[:, f, :], 1.0)
-
         a2 = [held.tile([P, EDGES], BF16, name="a2_%d" % t) for t in range(TERMS)]
 
-        with tc.psum_pool(name="psum_layers", bufs=3) as psum:
+        h_ev, h_e, h_e_bf, a1, forward_part = {}, {}, {}, {}, {}
+        with tc.psum_pool(name="psum_layers", bufs=2) as psum:
             plain_cols = held.tile([P, 2], F32, name="plain_cols")
             nc.vector.tensor_copy(plain_cols[:, 0:1], b3_col[:])
             nc.vector.tensor_copy(plain_cols[:, 1:2], b_out_col[:])
@@ -98,98 +103,135 @@ def tile_termedgempnnlayer_b_kernel(
             nc.vector.tensor_add(shifts[:, 1:2], shifts[:, 1:2], bias0_col[:])
             x_shift, y_shift = shifts[:, 0:1], shifts[:, 1:2]
 
-            for t in range(TERMS):
-                h_ev = loads.tile([P, IN_BLOCKS, EDGES], BF16, name="h_ev")
-                nc.sync.dma_start(h_ev[:], h_EV[t].rearrange("(a p) e -> p a e", p=P))
-                for h in range(HALVES):
-                    cols = slice(h * PIECE, (h + 1) * PIECE)
-                    sum1 = psum.tile([P, PIECE], F32, name="sum1")
-                    for a in range(IN_BLOCKS):
-                        nc.tensor.matmul(sum1[:], lhsT=w1_sb[:, a, :], rhs=h_ev[:, a, cols],
-                                         start=(a == 0), stop=(a == IN_BLOCKS - 1))
-                    a1 = work.tile([P, PIECE], BF16, name="a1")
-                    nc.scalar.activation(a1[:], sum1[:], ACT.Relu, bias=b1_col[:, 0:1])
-                    sum2 = psum.tile([P, PIECE], F32, name="sum2")
-                    nc.tensor.matmul(sum2[:], lhsT=w2_sb[:], rhs=a1[:], start=True, stop=True)
-                    nc.vector.tensor_scalar(a2[t][:, cols], sum2[:], b2_col[:, 0:1], 0.0, ALU.add, ALU.max)
+            w3_centred = held.tile([P, P], BF16, name="w3_centred")
+            centre_rows(w3_centred[:], w3_sb[:], 0.5)
 
-        h_e = []
-        for t in range(TERMS):
-            h_e.append(edges.tile([P, EDGES], F32, name="h_e"))
-            nc.sync.dma_start(h_e[t][:], h_E[:, t * EDGES:(t + 1) * EDGES])
+            def layer1(k):
+                t, cols = term_and_columns(k)
+                if k % HALVES == 0:
+                    h_ev[t] = loads.tile([P, IN_BLOCKS, EDGES], BF16, name="h_ev")
+                    nc.sync.dma_start(h_ev[t][:], h_EV[t].rearrange("(a p) e -> p a e", p=P))
+                    h_e[t] = loads.tile([P, EDGES], F32, name="h_e")
+                    nc.sync.dma_start(h_e[t][:], h_E[:, t * EDGES:(t + 1) * EDGES])
+                sum1 = psum.tile([P, PIECE], F32, name="sum1")
+                for a in range(IN_BLOCKS):
+                    nc.tensor.matmul(sum1[:], lhsT=w1_sb[:, a, :], rhs=h_ev[t][:, a, cols],
+                                     start=(a == 0), stop=(a == IN_BLOCKS - 1))
+                a1[k] = work.tile([P, PIECE], BF16, name="a1")
+                nc.scalar.activation(a1[k][:], sum1[:], ACT.Relu, bias=b1_col[:, 0:1])
+                h_e_bf[k] = work.tile([P, PIECE], BF16, name="h_e_bf")
+                nc.gpsimd.tensor_scalar(h_e_bf[k][:], h_e[t][:, cols], 1.0, 0.0, ALU.mult, ALU.add)
 
-        reverse_part = []
+            def layer2(k):
+                t, cols = term_and_columns(k)
+                sum2 = psum.tile([P, PIECE], F32, name="sum2")
+                nc.tensor.matmul(sum2[:], lhsT=w2_sb[:], rhs=a1[k][:], start=True, stop=True)
+                nc.vector.tensor_scalar(a2[t][:, cols], sum2[:], b2_col[:, 0:1], 0.0, ALU.add, ALU.max)
+
+            def forward_product(k):
+                t, cols = term_and_columns(k)
+                forward_sum = psum.tile([P, PIECE], F32, name="forward_sum")
+                nc.tensor.matmul(forward_sum[:], lhsT=minus_mean_bf[:], rhs=h_e_bf[k][:], start=True, stop=False)
+                nc.tensor.matmul(forward_sum[:], lhsT=w3_centred[:], rhs=a2[t][:, cols], start=False, stop=True)
+                forward_part[k] = pieces.tile([P, PIECE], F32, name="forward_part")
+                nc.vector.scalar_tensor_tensor(forward_part[k][:], forward_sum[:], x_shift, h_e[t][:, cols],
+                                               ALU.add, ALU.add)
+
+            for turn in range(PIECES + 2):
+                call_if_piece(layer1, turn)
+                call_if_piece(layer2, turn - 1)
+                call_if_piece(forward_product, turn - 2)
+
+        w_out_centred = held.tile([P, FF_BLOCKS, P], BF16, name="w_out_centred")
+        for f in range(FF_BLOCKS):
+            centre_rows(w_out_centred[:, f, :], w_out_sb[:, f, :], 1.0)
+
+        x_centred, x_squares = {}, {}
         with tc.psum_pool(name="psum_gather", bufs=8) as psum:
             for k in range(PIECES):
-                t, cols = k // HALVES, slice((k % HALVES) * PIECE, (k % HALVES + 1) * PIECE)
+                t, cols = term_and_columns(k)
                 looked_up = a2[t][:].indirect(offsets[:, k * (PIECE // 16):(k + 1) * (PIECE // 16)])
                 reverse_sum = psum.tile([P, PIECE], F32, name="reverse_sum")
                 nc.tensor.matmul(reverse_sum[:], lhsT=w3_centred[:], rhs=looked_up, start=True, stop=True)
-                reverse_part.append(pieces.tile([P, PIECE], F32, name="reverse_part"))
-                nc.vector.scalar_tensor_tensor(reverse_part[k][:], reverse_sum[:], x_shift, h_e[t][:, cols],
-                                               ALU.add, ALU.add)
+                x_centred[k] = pieces.tile([P, PIECE], F32, name="x_centred")
+                nc.vector.tensor_add(x_centred[k][:], reverse_sum[:], forward_part[k][:])
+                x_squares[k] = pieces.tile([P, PIECE], BF16, name="x_squares")
+                nc.scalar.activation(x_squares[k][:], x_centred[k][:], ACT.Square)
 
-        with tc.psum_pool(name="psum_rest", bufs=2) as psum:
+        x_inverse, u_less_bias, u_bf, hidden, y_centred, y_squares, y_inverse = {}, {}, {}, {}, {}, {}, {}
+        with tc.psum_pool(name="psum_rest", bufs=1) as psum:
 
-            def inverse_sigma(centred):
-                squares = work.tile([P, PIECE], BF16, name="squares")
-                nc.scalar.activation(squares[:], centred[:], ACT.Square)
-                square_sums = psum.tile([P, COL_BLOCKS], F32, name="square_sums", bufs=1)
+            def inverse_sigma(squares):
+                square_sums = psum.tile([P, COL_BLOCKS], F32, name="square_sums")
                 for b in range(COL_BLOCKS):
                     nc.tensor.matmul(square_sums[:, b:b + 1], lhsT=squares[:, b * P:(b + 1) * P], rhs=ones_col[:],
                                      start=True, stop=True)
                 sigma = small.tile([P, COL_BLOCKS], F32, name="sigma")
                 nc.scalar.activation(sigma[:], square_sums[:], ACT.Sqrt, bias=floor_col[:, 0:1], scale=1.0 / (P - 1))
-                nc.vector.tensor_scalar_add(sigma[:], sigma[:], EPS)
+                sigma_eps = small.tile([P, COL_BLOCKS], F32, name="sigma_eps")
+                nc.scalar.activation(sigma_eps[:], sigma[:], ACT.Identity, bias=eps_col[:, 0:1])
                 inverse = small.tile([P, COL_BLOCKS], F32, name="inverse")
-                nc.vector.reciprocal(inverse[:], sigma[:])
-                spread = psum.tile([P, PIECE], F32, name="spread")
+                nc.vector.reciprocal(inverse[:], sigma_eps[:])
+                return inverse
+
+            def spread(inverse):
+                spread_out = psum.tile([P, PIECE], F32, name="spread_out")
                 for b in range(COL_BLOCKS):
-                    nc.tensor.transpose(spread[:, b * P:(b + 1) * P], inverse[:, b:b + 1].to_broadcast([P, P]),
+                    nc.tensor.transpose(spread_out[:, b * P:(b + 1) * P], inverse[:, b:b + 1].to_broadcast([P, P]),
                                         identity[:])
-                return spread
+                return spread_out
 
-            for k in range(PIECES):
-                t, cols = k // HALVES, slice((k % HALVES) * PIECE, (k % HALVES + 1) * PIECE)
+            def x_sigma(k):
+                x_inverse[k] = inverse_sigma(x_squares[k])
 
-                h_e_bf = work.tile([P, PIECE], BF16, name="h_e_bf")
-                nc.gpsimd.tensor_scalar(h_e_bf[:], h_e[t][:, cols], 1.0, 0.0, ALU.mult, ALU.add)
-                forward_sum = psum.tile([P, PIECE], F32, name="forward_sum", tag="group")
-                nc.tensor.matmul(forward_sum[:], lhsT=minus_mean_bf[:], rhs=h_e_bf[:], start=True, stop=False)
-                nc.tensor.matmul(forward_sum[:], lhsT=w3_centred[:], rhs=a2[t][:, cols], start=False, stop=True)
-                x_centred = work.tile([P, PIECE], F32, name="x_centred")
-                nc.vector.tensor_add(x_centred[:], forward_sum[:], reverse_part[k][:])
-
-                x_scale = inverse_sigma(x_centred)
-                u_less_bias = work.tile([P, PIECE], F32, name="u_less_bias")
-                nc.vector.scalar_tensor_tensor(u_less_bias[:], x_centred[:], gain0_col[:, 0:1], x_scale[:],
+            def first_norm(k):
+                x_scale = spread(x_inverse[k])
+                u_less_bias[k] = work.tile([P, PIECE], F32, name="u_less_bias")
+                nc.vector.scalar_tensor_tensor(u_less_bias[k][:], x_centred[k][:], gain0_col[:, 0:1], x_scale[:],
                                                ALU.mult, ALU.mult)
-                u_bf = work.tile([P, PIECE], BF16, name="u_bf")
-                nc.gpsimd.tensor_scalar(u_bf[:], u_less_bias[:], 1.0, bias0_col[:, 0:1], ALU.mult, ALU.add)
+                u_bf[k] = work.tile([P, PIECE], BF16, name="u_bf")
+                nc.gpsimd.tensor_scalar(u_bf[k][:], u_less_bias[k][:], 1.0, bias0_col[:, 0:1], ALU.mult, ALU.add)
 
-                hidden = work.tile([P, FF_BLOCKS, PIECE], BF16, name="hidden")
+            def hidden_layer(k):
+                hidden[k] = work.tile([P, FF_BLOCKS, PIECE], BF16, name="hidden")
                 for f in range(FF_BLOCKS):
-                    hidden_sum = psum.tile([P, PIECE], F32, name="hidden_sum", bufs=3)
-                    nc.tensor.matmul(hidden_sum[:], lhsT=w_in_sb[:, f * P:(f + 1) * P], rhs=u_bf[:],
+                    hidden_sum = psum.tile([P, PIECE], F32, name="hidden_sum", bufs=FF_BLOCKS)
+                    nc.tensor.matmul(hidden_sum[:], lhsT=w_in_sb[:, f * P:(f + 1) * P], rhs=u_bf[k][:],
                                      start=True, stop=True)
-                    if f < FF_BLOCKS - 1:
-                        nc.scalar.activation(hidden[:, f, :], hidden_sum[:], ACT.Relu, bias=b_in_col[:, f:f + 1])
-                    else:
-                        nc.vector.tensor_scalar(hidden[:, f, :], hidden_sum[:], b_in_col[:, f:f + 1], 0.0,
+                    if f == 1:
+                        nc.vector.tensor_scalar(hidden[k][:, f, :], hidden_sum[:], b_in_col[:, f:f + 1], 0.0,
                                                 ALU.add, ALU.max)
+                    else:
+                        nc.scalar.activation(hidden[k][:, f, :], hidden_sum[:], ACT.Relu, bias=b_in_col[:, f:f + 1])
 
-                y_sum = psum.tile([P, PIECE], F32, name="y_sum", tag="group")
-                nc.tensor.matmul(y_sum[:], lhsT=minus_mean_bf[:], rhs=u_bf[:], start=True, stop=False)
+            def output_layer(k):
+                y_sum = psum.tile([P, PIECE], F32, name="y_sum", bufs=2)
+                nc.tensor.matmul(y_sum[:], lhsT=minus_mean_bf[:], rhs=u_bf[k][:], start=True, stop=False)
                 for f in range(FF_BLOCKS):
-                    nc.tensor.matmul(y_sum[:], lhsT=w_out_centred[:, f, :], rhs=hidden[:, f, :],
+                    nc.tensor.matmul(y_sum[:], lhsT=w_out_centred[:, f, :], rhs=hidden[k][:, f, :],
                                      start=False, stop=(f == FF_BLOCKS - 1))
-                y_centred = work.tile([P, PIECE], F32, name="y_centred")
-                nc.vector.scalar_tensor_tensor(y_centred[:], y_sum[:], y_shift, u_less_bias[:], ALU.add, ALU.add)
+                y_centred[k] = work.tile([P, PIECE], F32, name="y_centred")
+                nc.vector.scalar_tensor_tensor(y_centred[k][:], y_sum[:], y_shift, u_less_bias[k][:],
+                                               ALU.add, ALU.add)
+                y_squares[k] = work.tile([P, PIECE], BF16, name="y_squares")
+                nc.scalar.activation(y_squares[k][:], y_centred[k][:], ACT.Square)
 
-                y_scale = inverse_sigma(y_centred)
+            def y_sigma(k):
+                y_inverse[k] = inverse_sigma(y_squares[k])
+
+            def second_norm(k):
+                y_scale = spread(y_inverse[k])
                 scaled = work.tile([P, PIECE], F32, name="scaled")
-                nc.vector.scalar_tensor_tensor(scaled[:], y_centred[:], gain1_col[:, 0:1], y_scale[:],
+                nc.vector.scalar_tensor_tensor(scaled[:], y_centred[k][:], gain1_col[:, 0:1], y_scale[:],
                                                ALU.mult, ALU.mult)
                 result = work.tile([P, PIECE], F32, name="result")
                 nc.gpsimd.tensor_scalar(result[:], scaled[:], 1.0, bias1_col[:, 0:1], ALU.mult, ALU.add)
                 nc.sync.dma_start(out[:, k * PIECE:(k + 1) * PIECE], result[:])
+
+            for turn in range(PIECES + 2):
+                call_if_piece(x_sigma, turn)
+                call_if_piece(hidden_layer, turn - 1)
+                call_if_piece(first_norm, turn)
+                call_if_piece(y_sigma, turn - 2)
+                call_if_piece(output_layer, turn - 1)
+                call_if_piece(second_norm, turn - 2)

@@ -41,29 +41,43 @@ def tile_termedgempnnlayer_b_kernel(
         tc.tile_pool(name="work", bufs=4) as work,
         tc.tile_pool(name="small", bufs=4) as small,
     ):
-        offsets = held.tile([P, TERMS * EDGES // 16], U16, name="offsets")
-        nc.sync.dma_start(offsets[:], offs)
+        h_ev, h_e = {}, {}
+
+        def load_h_ev(t):
+            h_ev[t] = loads.tile([P, IN_BLOCKS, EDGES], BF16, name="h_ev")
+            nc.sync.dma_start(h_ev[t][:], h_EV[t].rearrange("(a p) e -> p a e", p=P))
+
+        def load_h_e(t):
+            h_e[t] = loads.tile([P, EDGES], F32, name="h_e")
+            nc.sync.dma_start(h_e[t][:], h_E[:, t * EDGES:(t + 1) * EDGES])
 
         def load_column(vector, blocks, name):
             column = held.tile([P, blocks], F32, name=name)
-            nc.scalar.dma_start(column[:], vector.rearrange("(a p) o -> p (a o)", p=P))
+            nc.sync.dma_start(column[:], vector.rearrange("(a p) o -> p (a o)", p=P))
             return column
 
+        def load_weights(weights, blocks, name):
+            tile = held.tile([P, blocks, P], BF16, name=name)
+            nc.sync.dma_start(tile[:], weights.rearrange("(a p) c -> p a c", p=P))
+            return tile
+
+        load_h_ev(0)
+        w1_sb = load_weights(w1, IN_BLOCKS, "w1_sb")
+        b1_col = load_column(b1, 1, "b1_col")
+        w2_sb = load_weights(w2, 1, "w2_sb")
+        b2_col = load_column(b2, 1, "b2_col")
+        w3_sb = load_weights(w3, 1, "w3_sb")
         b3_col = load_column(b3, 1, "b3_col")
         b_out_col = load_column(ffn_b_out, 1, "b_out_col")
+        load_h_e(0)
+        load_h_ev(1)
+        w_out_sb = load_weights(ffn_w_out, FF_BLOCKS, "w_out_sb")
         bias0_col = load_column(bias0, 1, "bias0_col")
-        w1_sb = held.tile([P, IN_BLOCKS, P], BF16, name="w1_sb")
-        nc.scalar.dma_start(w1_sb[:], w1.rearrange("(a p) c -> p a c", p=P))
-        b1_col = load_column(b1, 1, "b1_col")
-        w2_sb = held.tile([P, P], BF16, name="w2_sb")
-        nc.scalar.dma_start(w2_sb[:], w2)
-        b2_col = load_column(b2, 1, "b2_col")
-        w3_sb = held.tile([P, P], BF16, name="w3_sb")
-        nc.scalar.dma_start(w3_sb[:], w3)
+        load_h_e(1)
+        offsets = held.tile([P, TERMS * EDGES // 16], U16, name="offsets")
+        nc.sync.dma_start(offsets[:], offs)
         w_in_sb = held.tile([P, FF_BLOCKS * P], BF16, name="w_in_sb")
-        nc.scalar.dma_start(w_in_sb[:], ffn_w_in)
-        w_out_sb = held.tile([P, FF_BLOCKS, P], BF16, name="w_out_sb")
-        nc.scalar.dma_start(w_out_sb[:], ffn_w_out.rearrange("(a p) c -> p a c", p=P))
+        nc.sync.dma_start(w_in_sb[:], ffn_w_in)
         b_in_col = load_column(ffn_b_in, FF_BLOCKS, "b_in_col")
         gain0_col = load_column(gain0, 1, "gain0_col")
         gain1_col = load_column(gain1, 1, "gain1_col")
@@ -82,16 +96,20 @@ def tile_termedgempnnlayer_b_kernel(
         identity = held.tile([P, P], F32, name="identity")
         make_identity(nc, identity[:])
 
-        def centre_rows(centred, weights, scale):
-            row_sum = small.tile([P, 1], F32, name="row_sum")
-            nc.vector.reduce_sum(row_sum[:], weights, axis=AXIS.X)
-            minus_row_mean = small.tile([P, 1], F32, name="minus_row_mean")
-            nc.vector.tensor_scalar_mul(minus_row_mean[:], row_sum[:], -1.0 / P)
-            nc.vector.tensor_scalar(centred, weights, minus_row_mean[:, 0:1], scale, ALU.add, ALU.mult)
+        def centre_rows(weights, blocks, scale, name):
+            row_sums = small.tile([P, blocks], F32, name="row_sums")
+            nc.vector.reduce_sum(row_sums[:], weights[:], axis=AXIS.X)
+            minus_means = small.tile([P, blocks], F32, name="minus_means")
+            nc.vector.tensor_scalar_mul(minus_means[:], row_sums[:], -scale / P)
+            centred = held.tile([P, blocks, P], BF16, name=name)
+            nc.vector.scalar_tensor_tensor(centred[:], weights[:], scale,
+                                           minus_means[:].unsqueeze(2).to_broadcast([P, blocks, P]),
+                                           ALU.mult, ALU.add)
+            return centred
 
         a2 = [held.tile([P, EDGES], BF16, name="a2_%d" % t) for t in range(TERMS)]
 
-        h_ev, h_e, h_e_bf, a1, forward_part = {}, {}, {}, {}, {}
+        h_e_bf, a1, forward_part = {}, {}, {}
         with tc.psum_pool(name="psum_layers", bufs=2) as psum:
             plain_cols = held.tile([P, 2], F32, name="plain_cols")
             nc.vector.tensor_copy(plain_cols[:, 0:1], b3_col[:])
@@ -100,19 +118,15 @@ def tile_termedgempnnlayer_b_kernel(
             nc.tensor.matmul(minus_col_means[:], lhsT=minus_mean_f32[:], rhs=plain_cols[:], start=True, stop=True)
             shifts = held.tile([P, 2], F32, name="shifts")
             nc.vector.tensor_add(shifts[:], plain_cols[:], minus_col_means[:])
-            nc.vector.tensor_add(shifts[:, 1:2], shifts[:, 1:2], bias0_col[:])
             x_shift, y_shift = shifts[:, 0:1], shifts[:, 1:2]
 
-            w3_centred = held.tile([P, P], BF16, name="w3_centred")
-            centre_rows(w3_centred[:], w3_sb[:], 0.5)
+            w3_centred = centre_rows(w3_sb, 1, 0.5, "w3_centred")[:, 0, :]
 
             def layer1(k):
                 t, cols = term_and_columns(k)
-                if k % HALVES == 0:
-                    h_ev[t] = loads.tile([P, IN_BLOCKS, EDGES], BF16, name="h_ev")
-                    nc.sync.dma_start(h_ev[t][:], h_EV[t].rearrange("(a p) e -> p a e", p=P))
-                    h_e[t] = loads.tile([P, EDGES], F32, name="h_e")
-                    nc.sync.dma_start(h_e[t][:], h_E[:, t * EDGES:(t + 1) * EDGES])
+                if k % HALVES == 0 and t + 2 < TERMS:
+                    load_h_ev(t + 2)
+                    load_h_e(t + 2)
                 sum1 = psum.tile([P, PIECE], F32, name="sum1")
                 for a in range(IN_BLOCKS):
                     nc.tensor.matmul(sum1[:], lhsT=w1_sb[:, a, :], rhs=h_ev[t][:, a, cols],
@@ -125,26 +139,29 @@ def tile_termedgempnnlayer_b_kernel(
             def layer2(k):
                 t, cols = term_and_columns(k)
                 sum2 = psum.tile([P, PIECE], F32, name="sum2")
-                nc.tensor.matmul(sum2[:], lhsT=w2_sb[:], rhs=a1[k][:], start=True, stop=True)
+                nc.tensor.matmul(sum2[:], lhsT=w2_sb[:, 0, :], rhs=a1[k][:], start=True, stop=True)
                 nc.vector.tensor_scalar(a2[t][:, cols], sum2[:], b2_col[:, 0:1], 0.0, ALU.add, ALU.max)
 
             def forward_product(k):
                 t, cols = term_and_columns(k)
                 forward_sum = psum.tile([P, PIECE], F32, name="forward_sum")
                 nc.tensor.matmul(forward_sum[:], lhsT=minus_mean_bf[:], rhs=h_e_bf[k][:], start=True, stop=False)
-                nc.tensor.matmul(forward_sum[:], lhsT=w3_centred[:], rhs=a2[t][:, cols], start=False, stop=True)
+                nc.tensor.matmul(forward_sum[:], lhsT=w3_centred, rhs=a2[t][:, cols], start=False, stop=True)
                 forward_part[k] = pieces.tile([P, PIECE], F32, name="forward_part")
                 nc.vector.scalar_tensor_tensor(forward_part[k][:], forward_sum[:], x_shift, h_e[t][:, cols],
                                                ALU.add, ALU.add)
 
-            for turn in range(PIECES + 2):
+            def part1_turn(turn):
                 call_if_piece(layer1, turn)
                 call_if_piece(layer2, turn - 1)
                 call_if_piece(forward_product, turn - 2)
 
-        w_out_centred = held.tile([P, FF_BLOCKS, P], BF16, name="w_out_centred")
-        for f in range(FF_BLOCKS):
-            centre_rows(w_out_centred[:, f, :], w_out_sb[:, f, :], 1.0)
+            for turn in range(2):
+                part1_turn(turn)
+            w_out_centred = centre_rows(w_out_sb, FF_BLOCKS, 1.0, "w_out_centred")
+            nc.vector.tensor_add(y_shift, y_shift, bias0_col[:])
+            for turn in range(2, PIECES + 2):
+                part1_turn(turn)
 
         x_centred, x_squares = {}, {}
         with tc.psum_pool(name="psum_gather", bufs=8) as psum:
@@ -152,7 +169,7 @@ def tile_termedgempnnlayer_b_kernel(
                 t, cols = term_and_columns(k)
                 looked_up = a2[t][:].indirect(offsets[:, k * (PIECE // 16):(k + 1) * (PIECE // 16)])
                 reverse_sum = psum.tile([P, PIECE], F32, name="reverse_sum")
-                nc.tensor.matmul(reverse_sum[:], lhsT=w3_centred[:], rhs=looked_up, start=True, stop=True)
+                nc.tensor.matmul(reverse_sum[:], lhsT=w3_centred, rhs=looked_up, start=True, stop=True)
                 x_centred[k] = pieces.tile([P, PIECE], F32, name="x_centred")
                 nc.vector.tensor_add(x_centred[k][:], reverse_sum[:], forward_part[k][:])
                 x_squares[k] = pieces.tile([P, PIECE], BF16, name="x_squares")

@@ -17,6 +17,15 @@ COL_BLOCKS = PIECE // P
 EPS = 1e-6
 SQRT_FLOOR = 1e-30
 
+RING_BANKS = 5
+
+LAYER2_LAG = 1
+FORWARD_LAG = 2
+X_NORM_LAG = 5
+FFN_LAG = 6
+Y_NORM_LAG = 8
+TURNS = PIECES + Y_NORM_LAG
+
 FLOPS = 2 * TERMS * EDGES * P * (IN_BLOCKS * P + P + 2 * P + 2 * FF_BLOCKS * P)
 
 
@@ -24,8 +33,12 @@ def term_and_columns(k):
     return k // HALVES, slice((k % HALVES) * PIECE, (k % HALVES + 1) * PIECE)
 
 
+def is_piece(k):
+    return 0 <= k < PIECES
+
+
 def call_if_piece(step, k):
-    if 0 <= k < PIECES:
+    if is_piece(k):
         step(k)
 
 
@@ -36,19 +49,21 @@ def tile_termedgempnnlayer_b_kernel(
     nc = tc.nc
     with (
         tc.tile_pool(name="held", bufs=1) as held,
-        tc.tile_pool(name="loads", bufs=4) as loads,
-        tc.tile_pool(name="pieces", bufs=PIECES) as pieces,
+        tc.tile_pool(name="loads", bufs=5) as loads,
+        tc.tile_pool(name="long_work", bufs=6) as long_work,
         tc.tile_pool(name="work", bufs=4) as work,
         tc.tile_pool(name="small", bufs=4) as small,
+        tc.psum_pool(name="psum", bufs=1) as psum,
     ):
         h_ev, h_e = {}, {}
 
-        def load_h_ev(t):
+        def load_term(t):
             h_ev[t] = loads.tile([P, IN_BLOCKS, EDGES], BF16, name="h_ev")
             nc.sync.dma_start(h_ev[t][:], h_EV[t].rearrange("(a p) e -> p a e", p=P))
-
-        def load_h_e(t):
-            h_e[t] = loads.tile([P, EDGES], F32, name="h_e")
+            if t < 2:
+                h_e[t] = loads.tile([P, EDGES], F32, name="h_e_start", bufs=1)
+            else:
+                h_e[t] = loads.tile([P, EDGES], F32, name="h_e")
             nc.sync.dma_start(h_e[t][:], h_E[:, t * EDGES:(t + 1) * EDGES])
 
         def load_column(vector, blocks, name):
@@ -61,25 +76,23 @@ def tile_termedgempnnlayer_b_kernel(
             nc.sync.dma_start(tile[:], weights.rearrange("(a p) c -> p a c", p=P))
             return tile
 
-        load_h_ev(0)
         w1_sb = load_weights(w1, IN_BLOCKS, "w1_sb")
+        load_term(0)
         b1_col = load_column(b1, 1, "b1_col")
         w2_sb = load_weights(w2, 1, "w2_sb")
         b2_col = load_column(b2, 1, "b2_col")
         w3_sb = load_weights(w3, 1, "w3_sb")
         b3_col = load_column(b3, 1, "b3_col")
         b_out_col = load_column(ffn_b_out, 1, "b_out_col")
-        load_h_e(0)
-        load_h_ev(1)
-        w_out_sb = load_weights(ffn_w_out, FF_BLOCKS, "w_out_sb")
-        bias0_col = load_column(bias0, 1, "bias0_col")
-        load_h_e(1)
+        load_term(1)
         offsets = held.tile([P, TERMS * EDGES // 16], U16, name="offsets")
         nc.sync.dma_start(offsets[:], offs)
+        gain0_col = load_column(gain0, 1, "gain0_col")
+        bias0_col = load_column(bias0, 1, "bias0_col")
         w_in_sb = held.tile([P, FF_BLOCKS * P], BF16, name="w_in_sb")
         nc.sync.dma_start(w_in_sb[:], ffn_w_in)
         b_in_col = load_column(ffn_b_in, FF_BLOCKS, "b_in_col")
-        gain0_col = load_column(gain0, 1, "gain0_col")
+        w_out_sb = load_weights(ffn_w_out, FF_BLOCKS, "w_out_sb")
         gain1_col = load_column(gain1, 1, "gain1_col")
         bias1_col = load_column(bias1, 1, "bias1_col")
 
@@ -107,148 +120,151 @@ def tile_termedgempnnlayer_b_kernel(
                                            ALU.mult, ALU.add)
             return centred
 
-        a2 = [held.tile([P, EDGES], BF16, name="a2_%d" % t) for t in range(TERMS)]
+        def ring_bank(name):
+            return psum.tile([P, PIECE], F32, name=name, tag="ring", bufs=RING_BANKS)
 
-        h_e_bf, a1, forward_part = {}, {}, {}
-        with tc.psum_pool(name="psum_layers", bufs=2) as psum:
+        a2 = [held.tile([P, EDGES], BF16, name="a2_%d" % t) for t in range(TERMS)]
+        shifts = held.tile([P, 2], F32, name="shifts")
+        x_shift, y_shift = shifts[:, 0:1], shifts[:, 1:2]
+        prepared = {}
+
+        def prepare_message_constants():
             plain_cols = held.tile([P, 2], F32, name="plain_cols")
             nc.vector.tensor_copy(plain_cols[:, 0:1], b3_col[:])
             nc.vector.tensor_copy(plain_cols[:, 1:2], b_out_col[:])
-            minus_col_means = psum.tile([P, 2], F32, name="minus_col_means", bufs=1)
-            nc.tensor.matmul(minus_col_means[:], lhsT=minus_mean_f32[:], rhs=plain_cols[:], start=True, stop=True)
-            shifts = held.tile([P, 2], F32, name="shifts")
-            nc.vector.tensor_add(shifts[:], plain_cols[:], minus_col_means[:])
-            x_shift, y_shift = shifts[:, 0:1], shifts[:, 1:2]
+            minus_col_means = psum.tile([P, 2 * COL_BLOCKS], F32, name="minus_col_means", tag="square_sums")
+            nc.tensor.matmul(minus_col_means[:, 0:2], lhsT=minus_mean_f32[:], rhs=plain_cols[:], start=True, stop=True)
+            nc.vector.tensor_add(shifts[:], plain_cols[:], minus_col_means[:, 0:2])
+            prepared["w3"] = centre_rows(w3_sb, 1, 0.5, "w3_centred")[:, 0, :]
 
-            w3_centred = centre_rows(w3_sb, 1, 0.5, "w3_centred")[:, 0, :]
-
-            def layer1(k):
-                t, cols = term_and_columns(k)
-                if k % HALVES == 0 and t + 2 < TERMS:
-                    load_h_ev(t + 2)
-                    load_h_e(t + 2)
-                sum1 = psum.tile([P, PIECE], F32, name="sum1")
-                for a in range(IN_BLOCKS):
-                    nc.tensor.matmul(sum1[:], lhsT=w1_sb[:, a, :], rhs=h_ev[t][:, a, cols],
-                                     start=(a == 0), stop=(a == IN_BLOCKS - 1))
-                a1[k] = work.tile([P, PIECE], BF16, name="a1")
-                nc.scalar.activation(a1[k][:], sum1[:], ACT.Relu, bias=b1_col[:, 0:1])
-                h_e_bf[k] = work.tile([P, PIECE], BF16, name="h_e_bf")
-                nc.gpsimd.tensor_scalar(h_e_bf[k][:], h_e[t][:, cols], 1.0, 0.0, ALU.mult, ALU.add)
-
-            def layer2(k):
-                t, cols = term_and_columns(k)
-                sum2 = psum.tile([P, PIECE], F32, name="sum2")
-                nc.tensor.matmul(sum2[:], lhsT=w2_sb[:, 0, :], rhs=a1[k][:], start=True, stop=True)
-                nc.vector.tensor_scalar(a2[t][:, cols], sum2[:], b2_col[:, 0:1], 0.0, ALU.add, ALU.max)
-
-            def forward_product(k):
-                t, cols = term_and_columns(k)
-                forward_sum = psum.tile([P, PIECE], F32, name="forward_sum")
-                nc.tensor.matmul(forward_sum[:], lhsT=minus_mean_bf[:], rhs=h_e_bf[k][:], start=True, stop=False)
-                nc.tensor.matmul(forward_sum[:], lhsT=w3_centred, rhs=a2[t][:, cols], start=False, stop=True)
-                forward_part[k] = pieces.tile([P, PIECE], F32, name="forward_part")
-                nc.vector.scalar_tensor_tensor(forward_part[k][:], forward_sum[:], x_shift, h_e[t][:, cols],
-                                               ALU.add, ALU.add)
-
-            def part1_turn(turn):
-                call_if_piece(layer1, turn)
-                call_if_piece(layer2, turn - 1)
-                call_if_piece(forward_product, turn - 2)
-
-            for turn in range(2):
-                part1_turn(turn)
-            w_out_centred = centre_rows(w_out_sb, FF_BLOCKS, 1.0, "w_out_centred")
+        def prepare_ffn_constants():
+            prepared["w_out"] = centre_rows(w_out_sb, FF_BLOCKS, 1.0, "w_out_centred")
             nc.vector.tensor_add(y_shift, y_shift, bias0_col[:])
-            for turn in range(2, PIECES + 2):
-                part1_turn(turn)
 
-        x_centred, x_squares = {}, {}
-        with tc.psum_pool(name="psum_gather", bufs=8) as psum:
-            for k in range(PIECES):
-                t, cols = term_and_columns(k)
+        a1, h_e_bf, x_sum, x_centred, x_squares = {}, {}, {}, {}, {}
+        inverse, u_less_bias, u_bf, hidden, y_centred, y_squares = {}, {}, {}, {}, {}, {}
+
+        def layer1(k):
+            t, cols = term_and_columns(k)
+            sum1 = ring_bank("sum1")
+            for a in range(IN_BLOCKS):
+                nc.tensor.matmul(sum1[:], lhsT=w1_sb[:, a, :], rhs=h_ev[t][:, a, cols],
+                                 start=(a == 0), stop=(a == IN_BLOCKS - 1))
+            a1[k] = work.tile([P, PIECE], BF16, name="a1")
+            nc.scalar.activation(a1[k][:], sum1[:], ACT.Relu, bias=b1_col[:, 0:1])
+            h_e_bf[k] = work.tile([P, PIECE], BF16, name="h_e_bf")
+            nc.gpsimd.tensor_scalar(h_e_bf[k][:], h_e[t][:, cols], 1.0, 0.0, ALU.mult, ALU.add)
+
+        def layer2(k):
+            t, cols = term_and_columns(k)
+            sum2 = ring_bank("sum2")
+            nc.tensor.matmul(sum2[:], lhsT=w2_sb[:, 0, :], rhs=a1[k][:], start=True, stop=True)
+            nc.vector.tensor_scalar(a2[t][:, cols], sum2[:], b2_col[:, 0:1], 0.0, ALU.add, ALU.max)
+
+        def forward_products(t):
+            for k in range(t * HALVES, (t + 1) * HALVES):
+                cols = term_and_columns(k)[1]
+                x_sum[k] = psum.tile([P, PIECE], F32, name="x_sum", bufs=HALVES)
+                nc.tensor.matmul(x_sum[k][:], lhsT=minus_mean_bf[:], rhs=h_e_bf[k][:], start=True, stop=False)
+                nc.tensor.matmul(x_sum[k][:], lhsT=prepared["w3"], rhs=a2[t][:, cols], start=False, stop=False)
+
+        def reverse_products(t):
+            for k in range(t * HALVES, (t + 1) * HALVES):
                 looked_up = a2[t][:].indirect(offsets[:, k * (PIECE // 16):(k + 1) * (PIECE // 16)])
-                reverse_sum = psum.tile([P, PIECE], F32, name="reverse_sum")
-                nc.tensor.matmul(reverse_sum[:], lhsT=w3_centred, rhs=looked_up, start=True, stop=True)
-                x_centred[k] = pieces.tile([P, PIECE], F32, name="x_centred")
-                nc.vector.tensor_add(x_centred[k][:], reverse_sum[:], forward_part[k][:])
-                x_squares[k] = pieces.tile([P, PIECE], BF16, name="x_squares")
+                nc.tensor.matmul(x_sum[k][:], lhsT=prepared["w3"], rhs=looked_up, start=False, stop=True)
+            for k in range(t * HALVES, (t + 1) * HALVES):
+                cols = term_and_columns(k)[1]
+                x_centred[k] = long_work.tile([P, PIECE], F32, name="x_centred")
+                nc.vector.scalar_tensor_tensor(x_centred[k][:], x_sum[k][:], x_shift, h_e[t][:, cols],
+                                               ALU.add, ALU.add)
+                x_squares[k] = long_work.tile([P, PIECE], BF16, name="x_squares")
                 nc.scalar.activation(x_squares[k][:], x_centred[k][:], ACT.Square)
 
-        x_inverse, u_less_bias, u_bf, hidden, y_centred, y_squares, y_inverse = {}, {}, {}, {}, {}, {}, {}
-        with tc.psum_pool(name="psum_rest", bufs=1) as psum:
+        def inverse_sigmas(turn, kx, ky):
+            squares = [x_squares.get(kx), y_squares.get(ky)]
+            first = 0 if squares[0] is not None else COL_BLOCKS
+            last = 2 * COL_BLOCKS if squares[1] is not None else COL_BLOCKS
+            if first == last:
+                return
+            square_sums = psum.tile([P, 2 * COL_BLOCKS], F32, name="square_sums")
+            for c in range(first, last):
+                b = c % COL_BLOCKS
+                nc.tensor.matmul(square_sums[:, c:c + 1], lhsT=squares[c // COL_BLOCKS][:, b * P:(b + 1) * P],
+                                 rhs=ones_col[:], start=True, stop=True)
+            sigma = small.tile([P, 2 * COL_BLOCKS], F32, name="sigma")
+            nc.scalar.activation(sigma[:, first:last], square_sums[:, first:last], ACT.Sqrt,
+                                 bias=floor_col[:, 0:1], scale=1.0 / (P - 1))
+            sigma_eps = small.tile([P, 2 * COL_BLOCKS], F32, name="sigma_eps")
+            nc.scalar.activation(sigma_eps[:, first:last], sigma[:, first:last], ACT.Identity, bias=eps_col[:, 0:1])
+            inverse[turn] = small.tile([P, 2 * COL_BLOCKS], F32, name="inverse")
+            nc.vector.reciprocal(inverse[turn][:, first:last], sigma_eps[:, first:last])
 
-            def inverse_sigma(squares):
-                square_sums = psum.tile([P, COL_BLOCKS], F32, name="square_sums")
-                for b in range(COL_BLOCKS):
-                    nc.tensor.matmul(square_sums[:, b:b + 1], lhsT=squares[:, b * P:(b + 1) * P], rhs=ones_col[:],
-                                     start=True, stop=True)
-                sigma = small.tile([P, COL_BLOCKS], F32, name="sigma")
-                nc.scalar.activation(sigma[:], square_sums[:], ACT.Sqrt, bias=floor_col[:, 0:1], scale=1.0 / (P - 1))
-                sigma_eps = small.tile([P, COL_BLOCKS], F32, name="sigma_eps")
-                nc.scalar.activation(sigma_eps[:], sigma[:], ACT.Identity, bias=eps_col[:, 0:1])
-                inverse = small.tile([P, COL_BLOCKS], F32, name="inverse")
-                nc.vector.reciprocal(inverse[:], sigma_eps[:])
-                return inverse
+        def spread(inverse_columns):
+            spread_out = ring_bank("spread_out")
+            for b in range(COL_BLOCKS):
+                nc.tensor.transpose(spread_out[:, b * P:(b + 1) * P],
+                                    inverse_columns[:, b:b + 1].to_broadcast([P, P]), identity[:])
+            return spread_out
 
-            def spread(inverse):
-                spread_out = psum.tile([P, PIECE], F32, name="spread_out")
-                for b in range(COL_BLOCKS):
-                    nc.tensor.transpose(spread_out[:, b * P:(b + 1) * P], inverse[:, b:b + 1].to_broadcast([P, P]),
-                                        identity[:])
-                return spread_out
+        def first_norm(turn, k):
+            x_scale = spread(inverse[turn][:, 0:COL_BLOCKS])
+            u_less_bias[k] = work.tile([P, PIECE], F32, name="u_less_bias")
+            nc.vector.scalar_tensor_tensor(u_less_bias[k][:], x_centred[k][:], gain0_col[:, 0:1], x_scale[:],
+                                           ALU.mult, ALU.mult)
+            u_bf[k] = work.tile([P, PIECE], BF16, name="u_bf")
+            nc.scalar.activation(u_bf[k][:], u_less_bias[k][:], ACT.Identity, bias=bias0_col[:, 0:1])
 
-            def x_sigma(k):
-                x_inverse[k] = inverse_sigma(x_squares[k])
+        def hidden_layer(k):
+            hidden[k] = work.tile([P, FF_BLOCKS, PIECE], BF16, name="hidden")
+            for f in range(FF_BLOCKS):
+                hidden_sum = ring_bank("hidden_sum")
+                nc.tensor.matmul(hidden_sum[:], lhsT=w_in_sb[:, f * P:(f + 1) * P], rhs=u_bf[k][:],
+                                 start=True, stop=True)
+                if f % 2 == 1:
+                    nc.vector.tensor_scalar(hidden[k][:, f, :], hidden_sum[:], b_in_col[:, f:f + 1], 0.0,
+                                            ALU.add, ALU.max)
+                else:
+                    nc.scalar.activation(hidden[k][:, f, :], hidden_sum[:], ACT.Relu, bias=b_in_col[:, f:f + 1])
 
-            def first_norm(k):
-                x_scale = spread(x_inverse[k])
-                u_less_bias[k] = work.tile([P, PIECE], F32, name="u_less_bias")
-                nc.vector.scalar_tensor_tensor(u_less_bias[k][:], x_centred[k][:], gain0_col[:, 0:1], x_scale[:],
-                                               ALU.mult, ALU.mult)
-                u_bf[k] = work.tile([P, PIECE], BF16, name="u_bf")
-                nc.gpsimd.tensor_scalar(u_bf[k][:], u_less_bias[k][:], 1.0, bias0_col[:, 0:1], ALU.mult, ALU.add)
+        def output_layer(k):
+            y_sum = ring_bank("y_sum")
+            nc.tensor.matmul(y_sum[:], lhsT=minus_mean_bf[:], rhs=u_bf[k][:], start=True, stop=False)
+            for f in range(FF_BLOCKS):
+                nc.tensor.matmul(y_sum[:], lhsT=prepared["w_out"][:, f, :], rhs=hidden[k][:, f, :],
+                                 start=False, stop=(f == FF_BLOCKS - 1))
+            y_centred[k] = work.tile([P, PIECE], F32, name="y_centred")
+            nc.vector.scalar_tensor_tensor(y_centred[k][:], y_sum[:], y_shift, u_less_bias[k][:],
+                                           ALU.add, ALU.add)
+            y_squares[k] = work.tile([P, PIECE], BF16, name="y_squares")
+            nc.scalar.activation(y_squares[k][:], y_centred[k][:], ACT.Square)
 
-            def hidden_layer(k):
-                hidden[k] = work.tile([P, FF_BLOCKS, PIECE], BF16, name="hidden")
-                for f in range(FF_BLOCKS):
-                    hidden_sum = psum.tile([P, PIECE], F32, name="hidden_sum", bufs=FF_BLOCKS)
-                    nc.tensor.matmul(hidden_sum[:], lhsT=w_in_sb[:, f * P:(f + 1) * P], rhs=u_bf[k][:],
-                                     start=True, stop=True)
-                    if f == 1:
-                        nc.vector.tensor_scalar(hidden[k][:, f, :], hidden_sum[:], b_in_col[:, f:f + 1], 0.0,
-                                                ALU.add, ALU.max)
-                    else:
-                        nc.scalar.activation(hidden[k][:, f, :], hidden_sum[:], ACT.Relu, bias=b_in_col[:, f:f + 1])
+        def second_norm(turn, k):
+            y_scale = spread(inverse[turn][:, COL_BLOCKS:2 * COL_BLOCKS])
+            scaled = work.tile([P, PIECE], F32, name="scaled")
+            nc.vector.scalar_tensor_tensor(scaled[:], y_centred[k][:], gain1_col[:, 0:1], y_scale[:],
+                                           ALU.mult, ALU.mult)
+            result = work.tile([P, PIECE], F32, name="result")
+            nc.gpsimd.tensor_scalar(result[:], scaled[:], 1.0, bias1_col[:, 0:1], ALU.mult, ALU.add)
+            nc.sync.dma_start(out[:, k * PIECE:(k + 1) * PIECE], result[:])
 
-            def output_layer(k):
-                y_sum = psum.tile([P, PIECE], F32, name="y_sum", bufs=2)
-                nc.tensor.matmul(y_sum[:], lhsT=minus_mean_bf[:], rhs=u_bf[k][:], start=True, stop=False)
-                for f in range(FF_BLOCKS):
-                    nc.tensor.matmul(y_sum[:], lhsT=w_out_centred[:, f, :], rhs=hidden[k][:, f, :],
-                                     start=False, stop=(f == FF_BLOCKS - 1))
-                y_centred[k] = work.tile([P, PIECE], F32, name="y_centred")
-                nc.vector.scalar_tensor_tensor(y_centred[k][:], y_sum[:], y_shift, u_less_bias[k][:],
-                                               ALU.add, ALU.add)
-                y_squares[k] = work.tile([P, PIECE], BF16, name="y_squares")
-                nc.scalar.activation(y_squares[k][:], y_centred[k][:], ACT.Square)
-
-            def y_sigma(k):
-                y_inverse[k] = inverse_sigma(y_squares[k])
-
-            def second_norm(k):
-                y_scale = spread(y_inverse[k])
-                scaled = work.tile([P, PIECE], F32, name="scaled")
-                nc.vector.scalar_tensor_tensor(scaled[:], y_centred[k][:], gain1_col[:, 0:1], y_scale[:],
-                                               ALU.mult, ALU.mult)
-                result = work.tile([P, PIECE], F32, name="result")
-                nc.gpsimd.tensor_scalar(result[:], scaled[:], 1.0, bias1_col[:, 0:1], ALU.mult, ALU.add)
-                nc.sync.dma_start(out[:, k * PIECE:(k + 1) * PIECE], result[:])
-
-            for turn in range(PIECES + 2):
-                call_if_piece(x_sigma, turn)
-                call_if_piece(hidden_layer, turn - 1)
-                call_if_piece(first_norm, turn)
-                call_if_piece(y_sigma, turn - 2)
-                call_if_piece(output_layer, turn - 1)
-                call_if_piece(second_norm, turn - 2)
+        for turn in range(TURNS):
+            if turn % HALVES == 0 and turn // HALVES + 2 < TERMS:
+                load_term(turn // HALVES + 2)
+            inverse_sigmas(turn, turn - X_NORM_LAG, turn - Y_NORM_LAG)
+            call_if_piece(hidden_layer, turn - FFN_LAG)
+            call_if_piece(layer2, turn - LAYER2_LAG)
+            call_if_piece(layer1, turn)
+            if turn == 0:
+                prepare_message_constants()
+            if turn == FFN_LAG - 2:
+                prepare_ffn_constants()
+            since_forward = turn - FORWARD_LAG
+            if since_forward % HALVES == 0 and is_piece(since_forward):
+                forward_products(since_forward // HALVES)
+            if since_forward % HALVES == 1 and is_piece(since_forward):
+                reverse_products(since_forward // HALVES)
+            if is_piece(turn - X_NORM_LAG):
+                first_norm(turn, turn - X_NORM_LAG)
+            if is_piece(turn - Y_NORM_LAG):
+                second_norm(turn, turn - Y_NORM_LAG)
+            call_if_piece(output_layer, turn - FFN_LAG)

@@ -21,9 +21,9 @@ RING_BANKS = 5
 
 LAYER2_LAG = 1
 FORWARD_LAG = 2
-X_NORM_LAG = 5
-FFN_LAG = 6
-Y_NORM_LAG = 8
+X_NORM_LAG = 4
+FFN_LAG = 5
+Y_NORM_LAG = 7
 TURNS = PIECES + Y_NORM_LAG
 
 FLOPS = 2 * TERMS * EDGES * P * (IN_BLOCKS * P + P + 2 * P + 2 * FF_BLOCKS * P)
@@ -59,7 +59,9 @@ def tile_termedgempnnlayer_b_kernel(
 
         def load_term(t):
             h_ev[t] = loads.tile([P, IN_BLOCKS, EDGES], BF16, name="h_ev")
-            nc.sync.dma_start(h_ev[t][:], h_EV[t].rearrange("(a p) e -> p a e", p=P))
+            for half in range(HALVES):
+                cols = slice(half * PIECE, (half + 1) * PIECE)
+                nc.sync.dma_start(h_ev[t][:, :, cols], h_EV[t, :, cols].rearrange("(a p) e -> p a e", p=P))
             if t < 2:
                 h_e[t] = loads.tile([P, EDGES], F32, name="h_e_start", bufs=1)
             else:
@@ -77,10 +79,10 @@ def tile_termedgempnnlayer_b_kernel(
             return tile
 
         w1_sb = load_weights(w1, IN_BLOCKS, "w1_sb")
-        load_term(0)
         b1_col = load_column(b1, 1, "b1_col")
         w2_sb = load_weights(w2, 1, "w2_sb")
         b2_col = load_column(b2, 1, "b2_col")
+        load_term(0)
         w3_sb = load_weights(w3, 1, "w3_sb")
         b3_col = load_column(b3, 1, "b3_col")
         b_out_col = load_column(ffn_b_out, 1, "b_out_col")
@@ -161,17 +163,18 @@ def tile_termedgempnnlayer_b_kernel(
             nc.tensor.matmul(sum2[:], lhsT=w2_sb[:, 0, :], rhs=a1[k][:], start=True, stop=True)
             nc.vector.tensor_scalar(a2[t][:, cols], sum2[:], b2_col[:, 0:1], 0.0, ALU.add, ALU.max)
 
-        def forward_products(t):
-            for k in range(t * HALVES, (t + 1) * HALVES):
-                cols = term_and_columns(k)[1]
-                x_sum[k] = psum.tile([P, PIECE], F32, name="x_sum", bufs=HALVES)
-                nc.tensor.matmul(x_sum[k][:], lhsT=minus_mean_bf[:], rhs=h_e_bf[k][:], start=True, stop=False)
-                nc.tensor.matmul(x_sum[k][:], lhsT=prepared["w3"], rhs=a2[t][:, cols], start=False, stop=False)
+        def forward_product(k):
+            t, cols = term_and_columns(k)
+            x_sum[k] = psum.tile([P, PIECE], F32, name="x_sum", bufs=HALVES)
+            nc.tensor.matmul(x_sum[k][:], lhsT=minus_mean_bf[:], rhs=h_e_bf[k][:], start=True, stop=False)
+            nc.tensor.matmul(x_sum[k][:], lhsT=prepared["w3"], rhs=a2[t][:, cols], start=False, stop=False)
 
-        def reverse_products(t):
-            for k in range(t * HALVES, (t + 1) * HALVES):
-                looked_up = a2[t][:].indirect(offsets[:, k * (PIECE // 16):(k + 1) * (PIECE // 16)])
-                nc.tensor.matmul(x_sum[k][:], lhsT=prepared["w3"], rhs=looked_up, start=False, stop=True)
+        def reverse_product(k):
+            t = term_and_columns(k)[0]
+            looked_up = a2[t][:].indirect(offsets[:, k * (PIECE // 16):(k + 1) * (PIECE // 16)])
+            nc.tensor.matmul(x_sum[k][:], lhsT=prepared["w3"], rhs=looked_up, start=False, stop=True)
+
+        def centred_x(t):
             for k in range(t * HALVES, (t + 1) * HALVES):
                 cols = term_and_columns(k)[1]
                 x_centred[k] = long_work.tile([P, PIECE], F32, name="x_centred")
@@ -206,8 +209,7 @@ def tile_termedgempnnlayer_b_kernel(
                                     inverse_columns[:, b:b + 1].to_broadcast([P, P]), identity[:])
             return spread_out
 
-        def first_norm(turn, k):
-            x_scale = spread(inverse[turn][:, 0:COL_BLOCKS])
+        def first_norm(k, x_scale):
             u_less_bias[k] = work.tile([P, PIECE], F32, name="u_less_bias")
             nc.vector.scalar_tensor_tensor(u_less_bias[k][:], x_centred[k][:], gain0_col[:, 0:1], x_scale[:],
                                            ALU.mult, ALU.mult)
@@ -238,8 +240,7 @@ def tile_termedgempnnlayer_b_kernel(
             y_squares[k] = work.tile([P, PIECE], BF16, name="y_squares")
             nc.scalar.activation(y_squares[k][:], y_centred[k][:], ACT.Square)
 
-        def second_norm(turn, k):
-            y_scale = spread(inverse[turn][:, COL_BLOCKS:2 * COL_BLOCKS])
+        def second_norm(k, y_scale):
             scaled = work.tile([P, PIECE], F32, name="scaled")
             nc.vector.scalar_tensor_tensor(scaled[:], y_centred[k][:], gain1_col[:, 0:1], y_scale[:],
                                            ALU.mult, ALU.mult)
@@ -250,21 +251,31 @@ def tile_termedgempnnlayer_b_kernel(
         for turn in range(TURNS):
             if turn % HALVES == 0 and turn // HALVES + 2 < TERMS:
                 load_term(turn // HALVES + 2)
-            inverse_sigmas(turn, turn - X_NORM_LAG, turn - Y_NORM_LAG)
-            call_if_piece(hidden_layer, turn - FFN_LAG)
-            call_if_piece(layer2, turn - LAYER2_LAG)
-            call_if_piece(layer1, turn)
+            kx, kf, ky = turn - X_NORM_LAG, turn - FFN_LAG, turn - Y_NORM_LAG
+            layers_first = turn == FORWARD_LAG + HALVES + 1
+            if layers_first:
+                call_if_piece(layer2, turn - LAYER2_LAG)
+                call_if_piece(layer1, turn)
+            inverse_sigmas(turn, kx, ky)
+            call_if_piece(hidden_layer, kf)
+            if not layers_first:
+                call_if_piece(layer2, turn - LAYER2_LAG)
+                call_if_piece(layer1, turn)
             if turn == 0:
                 prepare_message_constants()
             if turn == FFN_LAG - 2:
                 prepare_ffn_constants()
             since_forward = turn - FORWARD_LAG
-            if since_forward % HALVES == 0 and is_piece(since_forward):
-                forward_products(since_forward // HALVES)
+            w3_product = forward_product if since_forward % HALVES == 0 else reverse_product
+            first_of_term = since_forward - since_forward % HALVES
+            call_if_piece(w3_product, first_of_term)
+            x_scale = spread(inverse[turn][:, 0:COL_BLOCKS]) if is_piece(kx) else None
+            call_if_piece(w3_product, first_of_term + 1)
+            y_scale = spread(inverse[turn][:, COL_BLOCKS:2 * COL_BLOCKS]) if is_piece(ky) else None
             if since_forward % HALVES == 1 and is_piece(since_forward):
-                reverse_products(since_forward // HALVES)
-            if is_piece(turn - X_NORM_LAG):
-                first_norm(turn, turn - X_NORM_LAG)
-            if is_piece(turn - Y_NORM_LAG):
-                second_norm(turn, turn - Y_NORM_LAG)
-            call_if_piece(output_layer, turn - FFN_LAG)
+                centred_x(since_forward // HALVES)
+            if is_piece(kx):
+                first_norm(kx, x_scale)
+            if is_piece(ky):
+                second_norm(ky, y_scale)
+            call_if_piece(output_layer, kf)

import concourse.mybir as mybir
from concourse.masks import make_identity

F32, BF16, U16 = mybir.dt.float32, mybir.dt.bfloat16, mybir.dt.uint16
ACT = mybir.ActivationFunctionType
ALU = mybir.AluOpType
AXIS = mybir.AxisListType

P = 128
TERMS, EDGES = 8, 1024
IN_BLOCKS = 3
FF_BLOCKS = 4
PIECE = 512
PIECES = TERMS * EDGES // PIECE
HALVES = EDGES // PIECE
COL_BLOCKS = PIECE // P
EPS = 1e-6
SQRT_FLOOR = 1e-30

RING_BANKS = 5

LAYER2_LAG = 1
FORWARD_LAG = 2
X_NORM_LAG = 4
FFN_LAG = 5
Y_NORM_LAG = 7
TURNS = PIECES + Y_NORM_LAG

FLOPS = 2 * TERMS * EDGES * P * (IN_BLOCKS * P + P + 2 * P + 2 * FF_BLOCKS * P)


def term_and_columns(k):
    return k // HALVES, slice((k % HALVES) * PIECE, (k % HALVES + 1) * PIECE)


def is_piece(k):
    return 0 <= k < PIECES


def call_if_piece(step, k):
    if is_piece(k):
        step(k)


def tile_termedgempnnlayer_b_kernel(
    tc, h_EV, h_E, w1, b1, w2, b2, w3, b3, ffn_w_in, ffn_b_in, ffn_w_out, ffn_b_out,
    gain0, bias0, gain1, bias1, offs, out,
):
    nc = tc.nc
    with (
        tc.tile_pool(name="held", bufs=1) as held,
        tc.tile_pool(name="loads", bufs=5) as loads,
        tc.tile_pool(name="long_work", bufs=6) as long_work,
        tc.tile_pool(name="work", bufs=4) as work,
        tc.tile_pool(name="small", bufs=4) as small,
        tc.psum_pool(name="psum", bufs=1) as psum,
    ):
        h_ev, h_e = {}, {}

        def load_term(t):
            h_ev[t] = loads.tile([P, IN_BLOCKS, EDGES], BF16, name="h_ev")
            for half in range(HALVES):
                cols = slice(half * PIECE, (half + 1) * PIECE)
                nc.sync.dma_start(h_ev[t][:, :, cols], h_EV[t, :, cols].rearrange("(a p) e -> p a e", p=P))
            if t < 2:
                h_e[t] = loads.tile([P, EDGES], F32, name="h_e_start", bufs=1)
            else:
                h_e[t] = loads.tile([P, EDGES], F32, name="h_e")
            nc.sync.dma_start(h_e[t][:], h_E[:, t * EDGES:(t + 1) * EDGES])

        def load_column(vector, blocks, name):
            column = held.tile([P, blocks], F32, name=name)
            nc.sync.dma_start(column[:], vector.rearrange("(a p) o -> p (a o)", p=P))
            return column

        def load_weights(weights, blocks, name):
            tile = held.tile([P, blocks, P], BF16, name=name)
            nc.sync.dma_start(tile[:], weights.rearrange("(a p) c -> p a c", p=P))
            return tile

        w1_sb = load_weights(w1, IN_BLOCKS, "w1_sb")
        b1_col = load_column(b1, 1, "b1_col")
        w2_sb = load_weights(w2, 1, "w2_sb")
        b2_col = load_column(b2, 1, "b2_col")
        load_term(0)
        w3_sb = load_weights(w3, 1, "w3_sb")
        b3_col = load_column(b3, 1, "b3_col")
        b_out_col = load_column(ffn_b_out, 1, "b_out_col")
        load_term(1)
        offsets = held.tile([P, TERMS * EDGES // 16], U16, name="offsets")
        nc.sync.dma_start(offsets[:], offs)
        gain0_col = load_column(gain0, 1, "gain0_col")
        bias0_col = load_column(bias0, 1, "bias0_col")
        w_in_sb = held.tile([P, FF_BLOCKS * P], BF16, name="w_in_sb")
        nc.sync.dma_start(w_in_sb[:], ffn_w_in)
        b_in_col = load_column(ffn_b_in, FF_BLOCKS, "b_in_col")
        w_out_sb = load_weights(ffn_w_out, FF_BLOCKS, "w_out_sb")
        gain1_col = load_column(gain1, 1, "gain1_col")
        bias1_col = load_column(bias1, 1, "bias1_col")

        minus_mean_bf = held.tile([P, P], BF16, name="minus_mean_bf")
        nc.vector.memset(minus_mean_bf[:], -1.0 / P)
        minus_mean_f32 = held.tile([P, P], F32, name="minus_mean_f32")
        nc.vector.memset(minus_mean_f32[:], -1.0 / P)
        ones_col = held.tile([P, 1], BF16, name="ones_col")
        nc.vector.memset(ones_col[:], 1.0)
        floor_col = held.tile([P, 1], F32, name="floor_col")
        nc.vector.memset(floor_col[:], SQRT_FLOOR)
        eps_col = held.tile([P, 1], F32, name="eps_col")
        nc.vector.memset(eps_col[:], EPS)
        identity = held.tile([P, P], F32, name="identity")
        make_identity(nc, identity[:])

        def centre_rows(weights, blocks, scale, name):
            row_sums = small.tile([P, blocks], F32, name="row_sums")
            nc.vector.reduce_sum(row_sums[:], weights[:], axis=AXIS.X)
            minus_means = small.tile([P, blocks], F32, name="minus_means")
            nc.vector.tensor_scalar_mul(minus_means[:], row_sums[:], -scale / P)
            centred = held.tile([P, blocks, P], BF16, name=name)
            nc.vector.scalar_tensor_tensor(centred[:], weights[:], scale,
                                           minus_means[:].unsqueeze(2).to_broadcast([P, blocks, P]),
                                           ALU.mult, ALU.add)
            return centred

        def ring_bank(name):
            return psum.tile([P, PIECE], F32, name=name, tag="ring", bufs=RING_BANKS)

        a2 = [held.tile([P, EDGES], BF16, name="a2_%d" % t) for t in range(TERMS)]
        shifts = held.tile([P, 2], F32, name="shifts")
        x_shift, y_shift = shifts[:, 0:1], shifts[:, 1:2]
        prepared = {}

        def prepare_message_constants():
            plain_cols = held.tile([P, 2], F32, name="plain_cols")
            nc.vector.tensor_copy(plain_cols[:, 0:1], b3_col[:])
            nc.vector.tensor_copy(plain_cols[:, 1:2], b_out_col[:])
            minus_col_means = psum.tile([P, 2 * COL_BLOCKS], F32, name="minus_col_means", tag="square_sums")
            nc.tensor.matmul(minus_col_means[:, 0:2], lhsT=minus_mean_f32[:], rhs=plain_cols[:], start=True, stop=True)
            nc.vector.tensor_add(shifts[:], plain_cols[:], minus_col_means[:, 0:2])
            prepared["w3"] = centre_rows(w3_sb, 1, 0.5, "w3_centred")[:, 0, :]

        def prepare_ffn_constants():
            prepared["w_out"] = centre_rows(w_out_sb, FF_BLOCKS, 1.0, "w_out_centred")
            nc.vector.tensor_add(y_shift, y_shift, bias0_col[:])

        a1, h_e_bf, x_sum, x_centred, x_squares = {}, {}, {}, {}, {}
        inverse, u_less_bias, u_bf, hidden, y_centred, y_squares = {}, {}, {}, {}, {}, {}

        def layer1(k):
            t, cols = term_and_columns(k)
            sum1 = ring_bank("sum1")
            for a in range(IN_BLOCKS):
                nc.tensor.matmul(sum1[:], lhsT=w1_sb[:, a, :], rhs=h_ev[t][:, a, cols],
                                 start=(a == 0), stop=(a == IN_BLOCKS - 1))
            a1[k] = work.tile([P, PIECE], BF16, name="a1")
            nc.scalar.activation(a1[k][:], sum1[:], ACT.Relu, bias=b1_col[:, 0:1])
            h_e_bf[k] = work.tile([P, PIECE], BF16, name="h_e_bf")
            nc.gpsimd.tensor_scalar(h_e_bf[k][:], h_e[t][:, cols], 1.0, 0.0, ALU.mult, ALU.add)

        def layer2(k):
            t, cols = term_and_columns(k)
            sum2 = ring_bank("sum2")
            nc.tensor.matmul(sum2[:], lhsT=w2_sb[:, 0, :], rhs=a1[k][:], start=True, stop=True)
            nc.vector.tensor_scalar(a2[t][:, cols], sum2[:], b2_col[:, 0:1], 0.0, ALU.add, ALU.max)

        def forward_product(k):
            t, cols = term_and_columns(k)
            x_sum[k] = psum.tile([P, PIECE], F32, name="x_sum", bufs=HALVES)
            nc.tensor.matmul(x_sum[k][:], lhsT=minus_mean_bf[:], rhs=h_e_bf[k][:], start=True, stop=False)
            nc.tensor.matmul(x_sum[k][:], lhsT=prepared["w3"], rhs=a2[t][:, cols], start=False, stop=False)

        def reverse_product(k):
            t = term_and_columns(k)[0]
            looked_up = a2[t][:].indirect(offsets[:, k * (PIECE // 16):(k + 1) * (PIECE // 16)])
            nc.tensor.matmul(x_sum[k][:], lhsT=prepared["w3"], rhs=looked_up, start=False, stop=True)

        def centred_x(t):
            for k in range(t * HALVES, (t + 1) * HALVES):
                cols = term_and_columns(k)[1]
                x_centred[k] = long_work.tile([P, PIECE], F32, name="x_centred")
                nc.vector.scalar_tensor_tensor(x_centred[k][:], x_sum[k][:], x_shift, h_e[t][:, cols],
                                               ALU.add, ALU.add)
                x_squares[k] = long_work.tile([P, PIECE], BF16, name="x_squares")
                nc.scalar.activation(x_squares[k][:], x_centred[k][:], ACT.Square)

        def inverse_sigmas(turn, kx, ky):
            squares = [x_squares.get(kx), y_squares.get(ky)]
            first = 0 if squares[0] is not None else COL_BLOCKS
            last = 2 * COL_BLOCKS if squares[1] is not None else COL_BLOCKS
            if first == last:
                return
            square_sums = psum.tile([P, 2 * COL_BLOCKS], F32, name="square_sums")
            for c in range(first, last):
                b = c % COL_BLOCKS
                nc.tensor.matmul(square_sums[:, c:c + 1], lhsT=squares[c // COL_BLOCKS][:, b * P:(b + 1) * P],
                                 rhs=ones_col[:], start=True, stop=True)
            sigma = small.tile([P, 2 * COL_BLOCKS], F32, name="sigma")
            nc.scalar.activation(sigma[:, first:last], square_sums[:, first:last], ACT.Sqrt,
                                 bias=floor_col[:, 0:1], scale=1.0 / (P - 1))
            sigma_eps = small.tile([P, 2 * COL_BLOCKS], F32, name="sigma_eps")
            nc.scalar.activation(sigma_eps[:, first:last], sigma[:, first:last], ACT.Identity, bias=eps_col[:, 0:1])
            inverse[turn] = small.tile([P, 2 * COL_BLOCKS], F32, name="inverse")
            nc.vector.reciprocal(inverse[turn][:, first:last], sigma_eps[:, first:last])

        def spread(inverse_columns):
            spread_out = ring_bank("spread_out")
            for b in range(COL_BLOCKS):
                nc.tensor.transpose(spread_out[:, b * P:(b + 1) * P],
                                    inverse_columns[:, b:b + 1].to_broadcast([P, P]), identity[:])
            return spread_out

        def first_norm(k, x_scale):
            u_less_bias[k] = work.tile([P, PIECE], F32, name="u_less_bias")
            nc.vector.scalar_tensor_tensor(u_less_bias[k][:], x_centred[k][:], gain0_col[:, 0:1], x_scale[:],
                                           ALU.mult, ALU.mult)
            u_bf[k] = work.tile([P, PIECE], BF16, name="u_bf")
            nc.scalar.activation(u_bf[k][:], u_less_bias[k][:], ACT.Identity, bias=bias0_col[:, 0:1])

        def hidden_layer(k):
            hidden[k] = work.tile([P, FF_BLOCKS, PIECE], BF16, name="hidden")
            for f in range(FF_BLOCKS):
                hidden_sum = ring_bank("hidden_sum")
                nc.tensor.matmul(hidden_sum[:], lhsT=w_in_sb[:, f * P:(f + 1) * P], rhs=u_bf[k][:],
                                 start=True, stop=True)
                if f % 2 == 1:
                    nc.vector.tensor_scalar(hidden[k][:, f, :], hidden_sum[:], b_in_col[:, f:f + 1], 0.0,
                                            ALU.add, ALU.max)
                else:
                    nc.scalar.activation(hidden[k][:, f, :], hidden_sum[:], ACT.Relu, bias=b_in_col[:, f:f + 1])

        def output_layer(k):
            y_sum = ring_bank("y_sum")
            nc.tensor.matmul(y_sum[:], lhsT=minus_mean_bf[:], rhs=u_bf[k][:], start=True, stop=False)
            for f in range(FF_BLOCKS):
                nc.tensor.matmul(y_sum[:], lhsT=prepared["w_out"][:, f, :], rhs=hidden[k][:, f, :],
                                 start=False, stop=(f == FF_BLOCKS - 1))
            y_centred[k] = work.tile([P, PIECE], F32, name="y_centred")
            nc.vector.scalar_tensor_tensor(y_centred[k][:], y_sum[:], y_shift, u_less_bias[k][:],
                                           ALU.add, ALU.add)
            y_squares[k] = work.tile([P, PIECE], BF16, name="y_squares")
            nc.scalar.activation(y_squares[k][:], y_centred[k][:], ACT.Square)

        def second_norm(k, y_scale):
            scaled = work.tile([P, PIECE], F32, name="scaled")
            nc.vector.scalar_tensor_tensor(scaled[:], y_centred[k][:], gain1_col[:, 0:1], y_scale[:],
                                           ALU.mult, ALU.mult)
            result = work.tile([P, PIECE], F32, name="result")
            nc.gpsimd.tensor_scalar(result[:], scaled[:], 1.0, bias1_col[:, 0:1], ALU.mult, ALU.add)
            nc.sync.dma_start(out[:, k * PIECE:(k + 1) * PIECE], result[:])

        for turn in range(TURNS):
            if turn % HALVES == 0 and turn // HALVES + 2 < TERMS:
                load_term(turn // HALVES + 2)
            kx, kf, ky = turn - X_NORM_LAG, turn - FFN_LAG, turn - Y_NORM_LAG
            layers_first = turn == FORWARD_LAG + HALVES + 1
            if layers_first:
                call_if_piece(layer2, turn - LAYER2_LAG)
                call_if_piece(layer1, turn)
            inverse_sigmas(turn, kx, ky)
            call_if_piece(hidden_layer, kf)
            if not layers_first:
                call_if_piece(layer2, turn - LAYER2_LAG)
                call_if_piece(layer1, turn)
            if turn == 0:
                prepare_message_constants()
            if turn == FFN_LAG - 2:
                prepare_ffn_constants()
            since_forward = turn - FORWARD_LAG
            w3_product = forward_product if since_forward % HALVES == 0 else reverse_product
            first_of_term = since_forward - since_forward % HALVES
            call_if_piece(w3_product, first_of_term)
            x_scale = spread(inverse[turn][:, 0:COL_BLOCKS]) if is_piece(kx) else None
            call_if_piece(w3_product, first_of_term + 1)
            y_scale = spread(inverse[turn][:, COL_BLOCKS:2 * COL_BLOCKS]) if is_piece(ky) else None
            if since_forward % HALVES == 1 and is_piece(since_forward):
                centred_x(since_forward // HALVES)
            if is_piece(kx):
                first_norm(kx, x_scale)
            if is_piece(ky):
                second_norm(ky, y_scale)
            call_if_piece(output_layer, kf)
